import numpy as np
import ml_dtypes


def mxq(x, axis, fmt="e4m3"):
    dtype, down = {"e4m3": (ml_dtypes.float8_e4m3fn, 7), "e5m2": (ml_dtypes.float8_e5m2, 14)}[fmt]
    v = np.moveaxis(np.asarray(x, np.float32).astype(ml_dtypes.bfloat16).astype(np.float64), axis, -1)
    blocks = v.reshape(v.shape[:-1] + (-1, 32))
    amax = np.abs(blocks).max(-1, keepdims=True)
    byte = np.maximum(np.where(amax > 0, np.frexp(amax)[1] - 1 + 127, 0) - down, 1)
    scale = np.exp2(byte - 127.0)
    codes = (blocks / scale).astype(np.float32).astype(dtype).astype(np.float64)
    return np.moveaxis((codes * scale).reshape(v.shape), -1, axis)


WIDE = False


def mx_kscale(k):
    if not WIDE:
        return np.ones(k)
    levels = np.array([20, -20, 10, -10, 0])
    a = np.random.permutation(np.resize(levels, k // 512 * 4)).reshape(k // 512, 4)
    idx = np.arange(k)
    return np.exp2(a[idx // 512, idx % 128 // 32])


BF16 = ml_dtypes.bfloat16


def bf(x):
    return np.asarray(x, np.float32).astype(BF16)


def f64(x):
    return np.asarray(x).astype(np.float64)


B, C, O, ROWS, COLS, KH, KW = 512, 64, 512, 4, 4, 4, 4
H, W, K = ROWS + KH - 1, COLS + KW - 1, C * KH * KW


def setup_inputs():
    s = mx_kscale(ROWS * COLS * O).reshape(ROWS, COLS, O)
    x = np.random.standard_normal((B, C, H, W))
    weight = np.random.standard_normal((ROWS, COLS, O, C, KH, KW)) / np.sqrt(K) / s[:, :, :, None, None, None]
    g = (np.random.standard_normal((B, O, ROWS, COLS))
         * np.exp2(np.random.randint(-12, 1, (B, 1, ROWS, COLS))) * 4.0
         * s.transpose(2, 0, 1)[None])
    return {"x": bf(x), "weight": bf(weight), "grad_out": bf(g)}


def reference(x, weight, grad_out):
    weight, g = f64(weight), f64(grad_out)
    rows, cols, o, c, kh, kw = weight.shape
    b = g.shape[0]
    gm = g.transpose(2, 3, 0, 1).reshape(rows * cols, b, o)
    wm = weight.reshape(rows * cols, o, c * kh * kw)
    d = mxq(gm, 2, "e5m2") @ mxq(wm, 1, "e4m3")
    d = d.reshape(rows, cols, b, c, kh, kw)
    gx = np.zeros((b, c, rows + kh - 1, cols + kw - 1))
    for i in range(rows):
        for j in range(cols):
            gx[:, :, i:i + kh, j:j + kw] += d[i, j]
    return gx

@@ -1,0 +1,231 @@
+from contextlib import ExitStack
+
+import concourse.mybir as mybir
+from concourse.masks import make_identity
+
+BF16 = mybir.dt.bfloat16
+F32 = mybir.dt.float32
+I32 = mybir.dt.int32
+U32 = mybir.dt.uint32
+U8 = mybir.dt.uint8
+E4M3X4 = mybir.dt.float8_e4m3fn_x4
+E5M2X4 = mybir.dt.float8_e5m2_x4
+ADD = mybir.AluOpType.add
+MULT = mybir.AluOpType.mult
+
+P = 128
+PACK = 4
+BATCH, C, O = 512, 64, 512
+ROWS, COLS, KH, KW = 4, 4, 4, 4
+H, W = ROWS + KH - 1, COLS + KW - 1
+B_TILES = BATCH // P
+POSITIONS = ROWS * COLS
+ROW_COLS = C * KW
+ROW_PAIRS = (H + 1) // 2
+
+COLUMN_ORDER = (0, 3, 1, 2)
+MATRICES = ROWS * COLS
+UNITS = COLS * B_TILES
+
+STRIP_ROWS = KH + 1
+RING = 10
+MULTIPLY_LAG = 5
+EMPTY_LAG = 6
+SHARED_FROM = 8
+GPSIMD_CHANNELS = 40
+
+FLOPS = 2 * POSITIONS * BATCH * O * C * KH * KW
+BYTES = 2 * POSITIONS * O * C * KH * KW + 2 * BATCH * O * POSITIONS + 4 * BATCH * C * H * W
+
+
+def tile_localconvolution_t_kernel(tc, x, weight, grad_out, out):
+    nc = tc.nc
+    with ExitStack() as ctx:
+        keep = ctx.enter_context(tc.tile_pool(name="keep", bufs=1))
+        big = ctx.enter_context(tc.tile_pool(name="big", bufs=B_TILES))
+        raw = ctx.enter_context(tc.tile_pool(name="raw", bufs=3))
+        grouped = ctx.enter_context(tc.tile_pool(name="grouped", bufs=4))
+        psum = ctx.enter_context(tc.psum_pool(name="psum", bufs=8))
+        ctx.enter_context(tc.manual_schedule())
+
+        identity = keep.tile([P, P], F32)
+        make_identity(nc, identity[:])
+
+        g_codes = keep.tile([P, B_TILES, POSITIONS * P], U32, align_bytes=64)
+        g_scales = keep.tile([P, B_TILES, POSITIONS * P], U8, align_bytes=64)
+        w_codes = keep.tile([P, (RING * STRIP_ROWS + 1) * ROW_COLS], U32, align_bytes=64)
+        w_scales = keep.tile([P, (RING * STRIP_ROWS + 1) * ROW_COLS], U8, align_bytes=64)
+
+        for plane in (w_codes, w_scales):
+            strips = plane[:, 0 : RING * STRIP_ROWS * ROW_COLS].rearrange(
+                "p (s r) -> p s r", s=RING
+            )
+            nc.vector.memset(strips[:, :, 0:ROW_COLS].bitcast(I32), 0)
+            nc.vector.memset(plane[:, RING * STRIP_ROWS * ROW_COLS :].bitcast(I32), 0)
+
+        def matrix_place(k):
+            return k % ROWS, COLUMN_ORDER[k // ROWS]
+
+        def strip_start(k):
+            return (k % RING) * STRIP_ROWS * ROW_COLS
+
+        def load_grad(bt):
+            g_raw = big.tile([P, O * POSITIONS], BF16, tag="big", name="g_raw")
+            rows = grad_out[bt * P : (bt + 1) * P]
+            nc.sync.dma_start(out=g_raw[:], in_=rows.rearrange("b o i j -> b (o i j)"))
+            return g_raw
+
+        def load_weight(k):
+            i, j = matrix_place(k)
+            w_raw = raw.tile([P, PACK, KH * ROW_COLS], BF16, tag="raw", name="w_raw")
+            nc.sync.dma_start(
+                out=w_raw[:], in_=weight[i, j].rearrange("(p t) c u v -> p t (c u v)", t=PACK)
+            )
+            return w_raw
+
+        def turn_grad(g_raw):
+            words = g_raw[:].bitcast(F32).rearrange(
+                "b (p t q) -> b p t q", t=PACK, q=POSITIONS // 2
+            )
+            halves = []
+            for half in range(2):
+                g_grouped = grouped.tile(
+                    [P, POSITIONS // 2, P, PACK], BF16, tag="grouped", name="g_grouped", align_bytes=64
+                )
+                for pair in range(POSITIONS // 4):
+                    q = half * (POSITIONS // 4) + pair
+                    turned = psum.tile([P, PACK, P], F32, tag="bank", name="turned")
+                    for t in range(PACK):
+                        nc.tensor.transpose(turned[:, t, :], words[:, :, t, q], identity[:])
+                    nc.scalar.copy(
+                        out=g_grouped[:, 2 * pair : 2 * pair + 2, :, :],
+                        in_=turned[:].bitcast(BF16).rearrange("p t (b e) -> p e b t", e=2),
+                    )
+                halves.append(g_grouped)
+            return halves
+
+        def quantise_grad(bt, half, g_grouped):
+            cols = slice(half * (POSITIONS // 2) * P, (half + 1) * (POSITIONS // 2) * P)
+            nc.vector.quantize_mx(
+                out=g_codes[:, bt, cols].bitcast(E5M2X4),
+                scales=g_scales[:, bt, cols],
+                in_=g_grouped[:].rearrange("p a b t -> p (a b t)"),
+            )
+
+        def regroup_weight(k, w_raw):
+            w_grouped = grouped.tile(
+                [P, KH, C, KW, PACK], BF16, tag="grouped", name="w_grouped", align_bytes=64
+            )
+            source = w_raw[:].rearrange("p t (c u v) -> p u c t v", u=KH, v=KW)
+            target = w_grouped[:].rearrange("p u c v t -> p u c t v")
+            vector_rows = KH if k < SHARED_FROM else KH // 2
+            nc.vector.tensor_copy(out=target[:, 0:vector_rows], in_=source[:, 0:vector_rows])
+            for u in range(vector_rows, KH):
+                nc.scalar.copy(out=target[:, u], in_=source[:, u])
+            return w_grouped
+
+        def quantise_weight(k, w_grouped):
+            first = strip_start(k) + ROW_COLS
+            cols = slice(first, first + KH * ROW_COLS)
+            nc.vector.quantize_mx(
+                out=w_codes[:, cols].bitcast(E4M3X4),
+                scales=w_scales[:, cols],
+                in_=w_grouped[:].rearrange("p u c v t -> p (u c v t)"),
+            )
+
+        def multiply(unit):
+            place, bt = divmod(unit, B_TILES)
+            banks = []
+            for rp in range(ROW_PAIRS):
+                windows = [i for i in range(ROWS) if -1 <= 2 * rp - i <= KH - 1]
+                bank = psum.tile([P, 2 * ROW_COLS], F32, tag="bank", name="bank")
+                for n, i in enumerate(windows):
+                    first = strip_start(place * ROWS + i) + (2 * rp - i + 1) * ROW_COLS
+                    position = i * COLS + COLUMN_ORDER[place]
+                    batch = slice(position * P, (position + 1) * P)
+                    nc.tensor.matmul_mx(
+                        out=bank[:],
+                        lhsT=g_codes[:, bt, batch].bitcast(E5M2X4),
+                        lhsT_scale=g_scales[:, bt, batch],
+                        rhs=w_codes[:, first : first + 2 * ROW_COLS].bitcast(E4M3X4),
+                        rhs_scale=w_scales[:, first : first + 2 * ROW_COLS],
+                        start=(n == 0),
+                        stop=(n == len(windows) - 1),
+                    )
+                banks.append(bank)
+            return banks
+
+        held = {}
+        written = 0
+        for j in COLUMN_ORDER:
+            held[j] = min(KW, max(0, written - j))
+            written = max(written, j + KW)
+
+        def empty(unit, banks, acc):
+            j = COLUMN_ORDER[unit // B_TILES]
+            for rp in range(ROW_PAIRS):
+                rows = min(2, H - 2 * rp)
+                product = banks[rp][:].rearrange("p (r c v) -> p r v c", r=2, v=KW)[:, 0:rows]
+                target = acc[:, 2 * rp : 2 * rp + rows, j : j + KW, :]
+                if held[j] > 0:
+                    nc.vector.tensor_tensor(
+                        out=target[:, :, 0 : held[j], :],
+                        in0=product[:, :, 0 : held[j], :],
+                        in1=target[:, :, 0 : held[j], :],
+                        op=ADD,
+                    )
+                if held[j] < KW:
+                    nc.scalar.copy(
+                        out=target[:, :, held[j] : KW, :], in_=product[:, :, held[j] : KW, :]
+                    )
+
+        def finish(bt, acc):
+            for first, count in ((0, GPSIMD_CHANNELS), (GPSIMD_CHANNELS, C - GPSIMD_CHANNELS)):
+                channels = slice(first, first + count)
+                result = raw.tile([P, count, H * W], F32, tag="raw", name="result")
+                source = acc[:, :, :, channels].rearrange("p h w c -> p c (h w)")
+                if first == 0:
+                    nc.gpsimd.tensor_scalar(
+                        out=result[:], in0=source, scalar1=1.0, scalar2=0.0, op0=MULT, op1=ADD
+                    )
+                else:
+                    nc.scalar.copy(out=result[:], in_=source)
+                nc.sync.dma_start(
+                    out=out[bt * P : (bt + 1) * P, channels].rearrange("b c h w -> b (c h w)"),
+                    in_=result[:].rearrange("p c s -> p (c s)"),
+                )
+
+        g_raws = {0: load_grad(0)}
+        w_raws = {0: load_weight(0), 1: load_weight(1)}
+        w_groupeds = {0: regroup_weight(0, w_raws[0])}
+        g_halves = {}
+        banks_of = {}
+        sums = {}
+        for step in range(UNITS + EMPTY_LAG):
+            unit = step - EMPTY_LAG
+            if unit >= 0:
+                bt = unit % B_TILES
+                if unit < B_TILES:
+                    sums[bt] = big.tile([P, H, W, C], F32, tag="big", name="acc")
+                empty(unit, banks_of[unit], sums[bt])
+                if unit >= UNITS - B_TILES:
+                    finish(bt, sums[bt])
+            if 1 <= step <= 2 * B_TILES:
+                bt, half = divmod(step - 1, 2)
+                quantise_grad(bt, half, g_halves[bt][half])
+            if step % 2 == 0:
+                bt = step // 2
+                if bt + 1 < B_TILES:
+                    g_raws[bt + 1] = load_grad(bt + 1)
+                for k in (step + 2, step + 3):
+                    if k < MATRICES:
+                        w_raws[k] = load_weight(k)
+                if bt < B_TILES:
+                    g_halves[bt] = turn_grad(g_raws[bt])
+            if step + 1 < MATRICES:
+                w_groupeds[step + 1] = regroup_weight(step + 1, w_raws[step + 1])
+            if step < MATRICES:
+                quantise_weight(step, w_groupeds[step])
+            unit = step - MULTIPLY_LAG
+            if 0 <= unit < UNITS:
+                banks_of[unit] = multiply(unit)

@@ -23,7 +23,7 @@ POSITIONS = ROWS * COLS
 ROW_COLS = C * KW
 ROW_PAIRS = (H + 1) // 2
 
-COLUMN_ORDER = (0, 3, 1, 2)
+COLUMN_ORDER = (0, 1, 2, 3)
 MATRICES = ROWS * COLS
 UNITS = COLS * B_TILES
 
@@ -182,7 +182,12 @@ def tile_localconvolution_t_kernel(tc, x, weight, grad_out, out):
         def finish(bt, acc):
             for first, count in ((0, GPSIMD_CHANNELS), (GPSIMD_CHANNELS, C - GPSIMD_CHANNELS)):
                 channels = slice(first, first + count)
-                result = raw.tile([P, count, H * W], F32, tag="raw", name="result")
+                if first == 0:
+                    result = grouped.tile(
+                        [P, count, H * W], F32, tag="grouped", name="result", align_bytes=64
+                    )
+                else:
+                    result = raw.tile([P, count, H * W], F32, tag="raw", name="result")
                 source = acc[:, :, :, channels].rearrange("p h w c -> p c (h w)")
                 if first == 0:
                     nc.gpsimd.tensor_scalar(
@@ -201,9 +206,9 @@ def tile_localconvolution_t_kernel(tc, x, weight, grad_out, out):
         g_halves = {}
         banks_of = {}
         sums = {}
-        for step in range(UNITS + EMPTY_LAG):
-            unit = step - EMPTY_LAG
-            if unit >= 0:
+        multiply_step = [n + (MULTIPLY_LAG if n < B_TILES else MULTIPLY_LAG - 1) for n in range(UNITS)]
+        for step in range(multiply_step[-1] + 2):
+            for unit in [n for n in range(UNITS) if multiply_step[n] + 1 == step]:
                 bt = unit % B_TILES
                 if unit < B_TILES:
                     sums[bt] = big.tile([P, H, W, C], F32, tag="big", name="acc")
@@ -226,6 +231,5 @@ def tile_localconvolution_t_kernel(tc, x, weight, grad_out, out):
                 w_groupeds[step + 1] = regroup_weight(step + 1, w_raws[step + 1])
             if step < MATRICES:
                 quantise_weight(step, w_groupeds[step])
-            unit = step - MULTIPLY_LAG
-            if 0 <= unit < UNITS:
+            for unit in [n for n in range(UNITS) if multiply_step[n] == step]:
                 banks_of[unit] = multiply(unit)

@@ -46,7 +46,6 @@ def tile_localconvolution_t_kernel(tc, x, weight, grad_out, out):
         raw = ctx.enter_context(tc.tile_pool(name="raw", bufs=3))
         grouped = ctx.enter_context(tc.tile_pool(name="grouped", bufs=4))
         psum = ctx.enter_context(tc.psum_pool(name="psum", bufs=8))
-        ctx.enter_context(tc.manual_schedule())
 
         identity = keep.tile([P, P], F32)
         make_identity(nc, identity[:])

@@ -32,7 +32,7 @@ RING = 10
 MULTIPLY_LAG = 5
 EMPTY_LAG = 6
 SHARED_FROM = 8
-GPSIMD_CHANNELS = 40
+FINISH_SHARES = (("vector", 16), ("scalar", 16), ("gpsimd", 32))
 
 FLOPS = 2 * POSITIONS * BATCH * O * C * KH * KW
 BYTES = 2 * POSITIONS * O * C * KH * KW + 2 * BATCH * O * POSITIONS + 4 * BATCH * C * H * W
@@ -43,7 +43,7 @@ def tile_localconvolution_t_kernel(tc, x, weight, grad_out, out):
     with ExitStack() as ctx:
         keep = ctx.enter_context(tc.tile_pool(name="keep", bufs=1))
         big = ctx.enter_context(tc.tile_pool(name="big", bufs=B_TILES))
-        raw = ctx.enter_context(tc.tile_pool(name="raw", bufs=3))
+        raw = ctx.enter_context(tc.tile_pool(name="raw", bufs=4))
         grouped = ctx.enter_context(tc.tile_pool(name="grouped", bufs=4))
         psum = ctx.enter_context(tc.psum_pool(name="psum", bufs=8))
 
@@ -179,19 +179,23 @@ def tile_localconvolution_t_kernel(tc, x, weight, grad_out, out):
                     )
 
         def finish(bt, acc):
-            for first, count in ((0, GPSIMD_CHANNELS), (GPSIMD_CHANNELS, C - GPSIMD_CHANNELS)):
+            first = 0
+            for engine, count in FINISH_SHARES:
                 channels = slice(first, first + count)
-                if first == 0:
+                first += count
+                if engine == "gpsimd":
+                    result = raw.tile([P, count, H * W], F32, tag="raw", name="result")
+                else:
                     result = grouped.tile(
                         [P, count, H * W], F32, tag="grouped", name="result", align_bytes=64
                     )
-                else:
-                    result = raw.tile([P, count, H * W], F32, tag="raw", name="result")
                 source = acc[:, :, :, channels].rearrange("p h w c -> p c (h w)")
-                if first == 0:
+                if engine == "gpsimd":
                     nc.gpsimd.tensor_scalar(
                         out=result[:], in0=source, scalar1=1.0, scalar2=0.0, op0=MULT, op1=ADD
                     )
+                elif engine == "vector":
+                    nc.vector.tensor_copy(out=result[:], in_=source)
                 else:
                     nc.scalar.copy(out=result[:], in_=source)
                 nc.sync.dma_start(

@@ -12,6 +12,8 @@ E4M3X4 = mybir.dt.float8_e4m3fn_x4
 E5M2X4 = mybir.dt.float8_e5m2_x4
 ADD = mybir.AluOpType.add
 MULT = mybir.AluOpType.mult
+MIN = mybir.AluOpType.min
+MAX = mybir.AluOpType.max
 
 P = 128
 PACK = 4
@@ -31,6 +33,7 @@ STRIP_ROWS = KH + 1
 RING = 10
 MULTIPLY_LAG = 5
 EMPTY_LAG = 6
+GPSIMD_FROM = 10
 SHARED_FROM = 8
 FINISH_SHARES = (("vector", 16), ("scalar", 16), ("gpsimd", 32))
 
@@ -45,6 +48,7 @@ def tile_localconvolution_t_kernel(tc, x, weight, grad_out, out):
         big = ctx.enter_context(tc.tile_pool(name="big", bufs=B_TILES))
         raw = ctx.enter_context(tc.tile_pool(name="raw", bufs=4))
         grouped = ctx.enter_context(tc.tile_pool(name="grouped", bufs=4))
+        flags = ctx.enter_context(tc.tile_pool(name="flags", bufs=2))
         psum = ctx.enter_context(tc.psum_pool(name="psum", bufs=8))
 
         identity = keep.tile([P, P], F32)
@@ -111,12 +115,24 @@ def tile_localconvolution_t_kernel(tc, x, weight, grad_out, out):
                 in_=g_grouped[:].rearrange("p a b t -> p (a b t)"),
             )
 
-        def regroup_weight(k, w_raw):
+        def regroup_weight(k, w_raw, go):
             w_grouped = grouped.tile(
                 [P, KH, C, KW, PACK], BF16, tag="grouped", name="w_grouped", align_bytes=64
             )
             source = w_raw[:].rearrange("p t (c u v) -> p u c t v", u=KH, v=KW)
             target = w_grouped[:].rearrange("p u c v t -> p u c t v")
+            if k >= GPSIMD_FROM:
+                nc.gpsimd.tensor_scalar(
+                    out=target[:, KH - 1], in0=source[:, KH - 1], scalar1=go[:, 0:1], scalar2=0.0,
+                    op0=MULT, op1=ADD,
+                )
+                nc.vector.tensor_copy(
+                    out=target[:, 0 : KH - 1, 0 : C // 2].rearrange("p u c t v -> p c u t v"),
+                    in_=source[:, 0 : KH - 1, 0 : C // 2].rearrange("p u c t v -> p c u t v"),
+                )
+                for u in range(KH - 1):
+                    nc.scalar.copy(out=target[:, u, C // 2 : C], in_=source[:, u, C // 2 : C])
+                return w_grouped
             vector_rows = KH if k < SHARED_FROM else KH // 2
             nc.vector.tensor_copy(out=target[:, 0:vector_rows], in_=source[:, 0:vector_rows])
             for u in range(vector_rows, KH):
@@ -162,6 +178,10 @@ def tile_localconvolution_t_kernel(tc, x, weight, grad_out, out):
 
         def empty(unit, banks, acc):
             j = COLUMN_ORDER[unit // B_TILES]
+            go = flags.tile([P, 1], F32, tag="go", name="go")
+            nc.vector.tensor_scalar(
+                out=go[:], in0=banks[0][:, 0:1], scalar1=1.0, scalar2=1.0, op0=MIN, op1=MAX
+            )
             for rp in range(ROW_PAIRS):
                 rows = min(2, H - 2 * rp)
                 product = banks[rp][:].rearrange("p (r c v) -> p r v c", r=2, v=KW)[:, 0:rows]
@@ -177,6 +197,7 @@ def tile_localconvolution_t_kernel(tc, x, weight, grad_out, out):
                     nc.scalar.copy(
                         out=target[:, :, held[j] : KW, :], in_=product[:, :, held[j] : KW, :]
                     )
+            return go
 
         def finish(bt, acc):
             first = 0
@@ -205,7 +226,8 @@ def tile_localconvolution_t_kernel(tc, x, weight, grad_out, out):
 
         g_raws = {0: load_grad(0)}
         w_raws = {0: load_weight(0), 1: load_weight(1)}
-        w_groupeds = {0: regroup_weight(0, w_raws[0])}
+        w_groupeds = {0: regroup_weight(0, w_raws[0], None)}
+        go = None
         g_halves = {}
         banks_of = {}
         sums = {}
@@ -215,7 +237,7 @@ def tile_localconvolution_t_kernel(tc, x, weight, grad_out, out):
                 bt = unit % B_TILES
                 if unit < B_TILES:
                     sums[bt] = big.tile([P, H, W, C], F32, tag="big", name="acc")
-                empty(unit, banks_of[unit], sums[bt])
+                go = empty(unit, banks_of[unit], sums[bt])
                 if unit >= UNITS - B_TILES:
                     finish(bt, sums[bt])
             if 1 <= step <= 2 * B_TILES:
@@ -231,7 +253,7 @@ def tile_localconvolution_t_kernel(tc, x, weight, grad_out, out):
                 if bt < B_TILES:
                     g_halves[bt] = turn_grad(g_raws[bt])
             if step + 1 < MATRICES:
-                w_groupeds[step + 1] = regroup_weight(step + 1, w_raws[step + 1])
+                w_groupeds[step + 1] = regroup_weight(step + 1, w_raws[step + 1], go)
             if step < MATRICES:
                 quantise_weight(step, w_groupeds[step])
             for unit in [n for n in range(UNITS) if multiply_step[n] == step]:

@@ -35,6 +35,7 @@ MULTIPLY_LAG = 5
 EMPTY_LAG = 6
 GPSIMD_FROM = 10
 SHARED_FROM = 8
+LINE = 4
 FINISH_SHARES = (("vector", 16), ("scalar", 16), ("gpsimd", 32))
 
 FLOPS = 2 * POSITIONS * BATCH * O * C * KH * KW
@@ -210,15 +211,16 @@ def tile_localconvolution_t_kernel(tc, x, weight, grad_out, out):
                     result = grouped.tile(
                         [P, count, H * W], F32, tag="grouped", name="result", align_bytes=64
                     )
-                source = acc[:, :, :, channels].rearrange("p h w c -> p c (h w)")
+                source = acc[:, :, :, channels].rearrange("p h w (g c) -> p g (h w) c", c=LINE)
+                target = result[:].rearrange("p (g c) s -> p g s c", c=LINE)
                 if engine == "gpsimd":
                     nc.gpsimd.tensor_scalar(
-                        out=result[:], in0=source, scalar1=1.0, scalar2=0.0, op0=MULT, op1=ADD
+                        out=target, in0=source, scalar1=1.0, scalar2=0.0, op0=MULT, op1=ADD
                     )
                 elif engine == "vector":
-                    nc.vector.tensor_copy(out=result[:], in_=source)
+                    nc.vector.tensor_copy(out=target, in_=source)
                 else:
-                    nc.scalar.copy(out=result[:], in_=source)
+                    nc.scalar.copy(out=target, in_=source)
                 nc.sync.dma_start(
                     out=out[bt * P : (bt + 1) * P, channels].rearrange("b c h w -> b (c h w)"),
                     in_=result[:].rearrange("p c s -> p (c s)"),

@@ -36,7 +36,7 @@ EMPTY_LAG = 6
 GPSIMD_FROM = 10
 SHARED_FROM = 8
 LINE = 4
-FINISH_SHARES = (("vector", 16), ("scalar", 16), ("gpsimd", 32))
+FINISH_SHARES = (("vector", 16), ("scalar", 24), ("vector", 24))
 
 FLOPS = 2 * POSITIONS * BATCH * O * C * KH * KW
 BYTES = 2 * POSITIONS * O * C * KH * KW + 2 * BATCH * O * POSITIONS + 4 * BATCH * C * H * W
@@ -205,7 +205,7 @@ def tile_localconvolution_t_kernel(tc, x, weight, grad_out, out):
             for engine, count in FINISH_SHARES:
                 channels = slice(first, first + count)
                 first += count
-                if engine == "gpsimd":
+                if engine == "scalar":
                     result = raw.tile([P, count, H * W], F32, tag="raw", name="result")
                 else:
                     result = grouped.tile(
@@ -213,11 +213,7 @@ def tile_localconvolution_t_kernel(tc, x, weight, grad_out, out):
                     )
                 source = acc[:, :, :, channels].rearrange("p h w (g c) -> p g (h w) c", c=LINE)
                 target = result[:].rearrange("p (g c) s -> p g s c", c=LINE)
-                if engine == "gpsimd":
-                    nc.gpsimd.tensor_scalar(
-                        out=target, in0=source, scalar1=1.0, scalar2=0.0, op0=MULT, op1=ADD
-                    )
-                elif engine == "vector":
+                if engine == "vector":
                     nc.vector.tensor_copy(out=target, in_=source)
                 else:
                     nc.scalar.copy(out=target, in_=source)

@@ -35,6 +35,7 @@ MULTIPLY_LAG = 5
 EMPTY_LAG = 6
 GPSIMD_FROM = 10
 SHARED_FROM = 8
+AHEAD_UNIT = UNITS - B_TILES
 LINE = 4
 FINISH_SHARES = (("vector", 16), ("scalar", 24), ("vector", 24))
 
@@ -149,26 +150,25 @@ def tile_localconvolution_t_kernel(tc, x, weight, grad_out, out):
                 in_=w_grouped[:].rearrange("p u c v t -> p (u c v t)"),
             )
 
-        def multiply(unit):
+        def multiply(unit, first_window, last_window, banks):
             place, bt = divmod(unit, B_TILES)
-            banks = []
             for rp in range(ROW_PAIRS):
                 windows = [i for i in range(ROWS) if -1 <= 2 * rp - i <= KH - 1]
-                bank = psum.tile([P, 2 * ROW_COLS], F32, tag="bank", name="bank")
-                for n, i in enumerate(windows):
+                for i in [i for i in windows if first_window <= i <= last_window]:
+                    if i == windows[0]:
+                        banks[rp] = psum.tile([P, 2 * ROW_COLS], F32, tag="bank", name="bank")
                     first = strip_start(place * ROWS + i) + (2 * rp - i + 1) * ROW_COLS
                     position = i * COLS + COLUMN_ORDER[place]
                     batch = slice(position * P, (position + 1) * P)
                     nc.tensor.matmul_mx(
-                        out=bank[:],
+                        out=banks[rp][:],
                         lhsT=g_codes[:, bt, batch].bitcast(E5M2X4),
                         lhsT_scale=g_scales[:, bt, batch],
                         rhs=w_codes[:, first : first + 2 * ROW_COLS].bitcast(E4M3X4),
                         rhs_scale=w_scales[:, first : first + 2 * ROW_COLS],
-                        start=(n == 0),
-                        stop=(n == len(windows) - 1),
+                        start=(i == windows[0]),
+                        stop=(i == windows[-1]),
                     )
-                banks.append(bank)
             return banks
 
         held = {}
@@ -255,4 +255,9 @@ def tile_localconvolution_t_kernel(tc, x, weight, grad_out, out):
             if step < MATRICES:
                 quantise_weight(step, w_groupeds[step])
             for unit in [n for n in range(UNITS) if multiply_step[n] == step]:
-                banks_of[unit] = multiply(unit)
+                if unit == AHEAD_UNIT:
+                    multiply(unit, ROWS - 1, ROWS - 1, banks_of[unit])
+                else:
+                    banks_of[unit] = multiply(unit, 0, ROWS - 1, {})
+            if step + 1 == multiply_step[AHEAD_UNIT]:
+                banks_of[AHEAD_UNIT] = multiply(AHEAD_UNIT, 0, ROWS - 2, {})

@@ -36,6 +36,7 @@ EMPTY_LAG = 6
 GPSIMD_FROM = 10
 SHARED_FROM = 8
 AHEAD_UNIT = UNITS - B_TILES
+LATE_VECTOR_CHANNELS = 24
 LINE = 4
 FINISH_SHARES = (("vector", 16), ("scalar", 24), ("vector", 24))
 
@@ -129,11 +130,13 @@ def tile_localconvolution_t_kernel(tc, x, weight, grad_out, out):
                     op0=MULT, op1=ADD,
                 )
                 nc.vector.tensor_copy(
-                    out=target[:, 0 : KH - 1, 0 : C // 2].rearrange("p u c t v -> p c u t v"),
-                    in_=source[:, 0 : KH - 1, 0 : C // 2].rearrange("p u c t v -> p c u t v"),
+                    out=target[:, 0 : KH - 1, 0:LATE_VECTOR_CHANNELS].rearrange("p u c t v -> p c u t v"),
+                    in_=source[:, 0 : KH - 1, 0:LATE_VECTOR_CHANNELS].rearrange("p u c t v -> p c u t v"),
                 )
                 for u in range(KH - 1):
-                    nc.scalar.copy(out=target[:, u, C // 2 : C], in_=source[:, u, C // 2 : C])
+                    nc.scalar.copy(
+                        out=target[:, u, LATE_VECTOR_CHANNELS:C], in_=source[:, u, LATE_VECTOR_CHANNELS:C]
+                    )
                 return w_grouped
             vector_rows = KH if k < SHARED_FROM else KH // 2
             nc.vector.tensor_copy(out=target[:, 0:vector_rows], in_=source[:, 0:vector_rows])
@@ -177,12 +180,14 @@ def tile_localconvolution_t_kernel(tc, x, weight, grad_out, out):
             held[j] = min(KW, max(0, written - j))
             written = max(written, j + KW)
 
-        def empty(unit, banks, acc):
+        def empty(unit, banks, acc, flag):
             j = COLUMN_ORDER[unit // B_TILES]
-            go = flags.tile([P, 1], F32, tag="go", name="go")
-            nc.vector.tensor_scalar(
-                out=go[:], in0=banks[0][:, 0:1], scalar1=1.0, scalar2=1.0, op0=MIN, op1=MAX
-            )
+            go = None
+            if flag:
+                go = flags.tile([P, 1], F32, tag="go", name="go")
+                nc.vector.tensor_scalar(
+                    out=go[:], in0=banks[0][:, 0:1], scalar1=1.0, scalar2=1.0, op0=MIN, op1=MAX
+                )
             for rp in range(ROW_PAIRS):
                 rows = min(2, H - 2 * rp)
                 product = banks[rp][:].rearrange("p (r c v) -> p r v c", r=2, v=KW)[:, 0:rows]
@@ -235,7 +240,7 @@ def tile_localconvolution_t_kernel(tc, x, weight, grad_out, out):
                 bt = unit % B_TILES
                 if unit < B_TILES:
                     sums[bt] = big.tile([P, H, W, C], F32, tag="big", name="acc")
-                go = empty(unit, banks_of[unit], sums[bt])
+                go = empty(unit, banks_of[unit], sums[bt], GPSIMD_FROM <= step + 1 < MATRICES)
                 if unit >= UNITS - B_TILES:
                     finish(bt, sums[bt])
             if 1 <= step <= 2 * B_TILES:

from contextlib import ExitStack

import concourse.mybir as mybir
from concourse.masks import make_identity

BF16 = mybir.dt.bfloat16
F32 = mybir.dt.float32
I32 = mybir.dt.int32
U32 = mybir.dt.uint32
U8 = mybir.dt.uint8
E4M3X4 = mybir.dt.float8_e4m3fn_x4
E5M2X4 = mybir.dt.float8_e5m2_x4
ADD = mybir.AluOpType.add
MULT = mybir.AluOpType.mult
MIN = mybir.AluOpType.min
MAX = mybir.AluOpType.max

P = 128
PACK = 4
BATCH, C, O = 512, 64, 512
ROWS, COLS, KH, KW = 4, 4, 4, 4
H, W = ROWS + KH - 1, COLS + KW - 1
B_TILES = BATCH // P
POSITIONS = ROWS * COLS
ROW_COLS = C * KW
ROW_PAIRS = (H + 1) // 2

COLUMN_ORDER = (0, 1, 2, 3)
MATRICES = ROWS * COLS
UNITS = COLS * B_TILES

STRIP_ROWS = KH + 1
RING = 10
MULTIPLY_LAG = 5
EMPTY_LAG = 6
GPSIMD_FROM = 10
SHARED_FROM = 8
AHEAD_UNIT = UNITS - B_TILES
LATE_VECTOR_CHANNELS = 24
LINE = 4
FINISH_SHARES = (("vector", 16), ("scalar", 24), ("vector", 24))

FLOPS = 2 * POSITIONS * BATCH * O * C * KH * KW
BYTES = 2 * POSITIONS * O * C * KH * KW + 2 * BATCH * O * POSITIONS + 4 * BATCH * C * H * W


def tile_localconvolution_t_kernel(tc, x, weight, grad_out, out):
    nc = tc.nc
    with ExitStack() as ctx:
        keep = ctx.enter_context(tc.tile_pool(name="keep", bufs=1))
        big = ctx.enter_context(tc.tile_pool(name="big", bufs=B_TILES))
        raw = ctx.enter_context(tc.tile_pool(name="raw", bufs=4))
        grouped = ctx.enter_context(tc.tile_pool(name="grouped", bufs=4))
        flags = ctx.enter_context(tc.tile_pool(name="flags", bufs=2))
        psum = ctx.enter_context(tc.psum_pool(name="psum", bufs=8))

        identity = keep.tile([P, P], F32)
        make_identity(nc, identity[:])

        g_codes = keep.tile([P, B_TILES, POSITIONS * P], U32, align_bytes=64)
        g_scales = keep.tile([P, B_TILES, POSITIONS * P], U8, align_bytes=64)
        w_codes = keep.tile([P, (RING * STRIP_ROWS + 1) * ROW_COLS], U32, align_bytes=64)
        w_scales = keep.tile([P, (RING * STRIP_ROWS + 1) * ROW_COLS], U8, align_bytes=64)

        for plane in (w_codes, w_scales):
            strips = plane[:, 0 : RING * STRIP_ROWS * ROW_COLS].rearrange(
                "p (s r) -> p s r", s=RING
            )
            nc.vector.memset(strips[:, :, 0:ROW_COLS].bitcast(I32), 0)
            nc.vector.memset(plane[:, RING * STRIP_ROWS * ROW_COLS :].bitcast(I32), 0)

        def matrix_place(k):
            return k % ROWS, COLUMN_ORDER[k // ROWS]

        def strip_start(k):
            return (k % RING) * STRIP_ROWS * ROW_COLS

        def load_grad(bt):
            g_raw = big.tile([P, O * POSITIONS], BF16, tag="big", name="g_raw")
            rows = grad_out[bt * P : (bt + 1) * P]
            nc.sync.dma_start(out=g_raw[:], in_=rows.rearrange("b o i j -> b (o i j)"))
            return g_raw

        def load_weight(k):
            i, j = matrix_place(k)
            w_raw = raw.tile([P, PACK, KH * ROW_COLS], BF16, tag="raw", name="w_raw")
            nc.sync.dma_start(
                out=w_raw[:], in_=weight[i, j].rearrange("(p t) c u v -> p t (c u v)", t=PACK)
            )
            return w_raw

        def turn_grad(g_raw):
            words = g_raw[:].bitcast(F32).rearrange(
                "b (p t q) -> b p t q", t=PACK, q=POSITIONS // 2
            )
            halves = []
            for half in range(2):
                g_grouped = grouped.tile(
                    [P, POSITIONS // 2, P, PACK], BF16, tag="grouped", name="g_grouped", align_bytes=64
                )
                for pair in range(POSITIONS // 4):
                    q = half * (POSITIONS // 4) + pair
                    turned = psum.tile([P, PACK, P], F32, tag="bank", name="turned")
                    for t in range(PACK):
                        nc.tensor.transpose(turned[:, t, :], words[:, :, t, q], identity[:])
                    nc.scalar.copy(
                        out=g_grouped[:, 2 * pair : 2 * pair + 2, :, :],
                        in_=turned[:].bitcast(BF16).rearrange("p t (b e) -> p e b t", e=2),
                    )
                halves.append(g_grouped)
            return halves

        def quantise_grad(bt, half, g_grouped):
            cols = slice(half * (POSITIONS // 2) * P, (half + 1) * (POSITIONS // 2) * P)
            nc.vector.quantize_mx(
                out=g_codes[:, bt, cols].bitcast(E5M2X4),
                scales=g_scales[:, bt, cols],
                in_=g_grouped[:].rearrange("p a b t -> p (a b t)"),
            )

        def regroup_weight(k, w_raw, go):
            w_grouped = grouped.tile(
                [P, KH, C, KW, PACK], BF16, tag="grouped", name="w_grouped", align_bytes=64
            )
            source = w_raw[:].rearrange("p t (c u v) -> p u c t v", u=KH, v=KW)
            target = w_grouped[:].rearrange("p u c v t -> p u c t v")
            if k >= GPSIMD_FROM:
                nc.gpsimd.tensor_scalar(
                    out=target[:, KH - 1], in0=source[:, KH - 1], scalar1=go[:, 0:1], scalar2=0.0,
                    op0=MULT, op1=ADD,
                )
                nc.vector.tensor_copy(
                    out=target[:, 0 : KH - 1, 0:LATE_VECTOR_CHANNELS].rearrange("p u c t v -> p c u t v"),
                    in_=source[:, 0 : KH - 1, 0:LATE_VECTOR_CHANNELS].rearrange("p u c t v -> p c u t v"),
                )
                for u in range(KH - 1):
                    nc.scalar.copy(
                        out=target[:, u, LATE_VECTOR_CHANNELS:C], in_=source[:, u, LATE_VECTOR_CHANNELS:C]
                    )
                return w_grouped
            vector_rows = KH if k < SHARED_FROM else KH // 2
            nc.vector.tensor_copy(out=target[:, 0:vector_rows], in_=source[:, 0:vector_rows])
            for u in range(vector_rows, KH):
                nc.scalar.copy(out=target[:, u], in_=source[:, u])
            return w_grouped

        def quantise_weight(k, w_grouped):
            first = strip_start(k) + ROW_COLS
            cols = slice(first, first + KH * ROW_COLS)
            nc.vector.quantize_mx(
                out=w_codes[:, cols].bitcast(E4M3X4),
                scales=w_scales[:, cols],
                in_=w_grouped[:].rearrange("p u c v t -> p (u c v t)"),
            )

        def multiply(unit, first_window, last_window, banks):
            place, bt = divmod(unit, B_TILES)
            for rp in range(ROW_PAIRS):
                windows = [i for i in range(ROWS) if -1 <= 2 * rp - i <= KH - 1]
                for i in [i for i in windows if first_window <= i <= last_window]:
                    if i == windows[0]:
                        banks[rp] = psum.tile([P, 2 * ROW_COLS], F32, tag="bank", name="bank")
                    first = strip_start(place * ROWS + i) + (2 * rp - i + 1) * ROW_COLS
                    position = i * COLS + COLUMN_ORDER[place]
                    batch = slice(position * P, (position + 1) * P)
                    nc.tensor.matmul_mx(
                        out=banks[rp][:],
                        lhsT=g_codes[:, bt, batch].bitcast(E5M2X4),
                        lhsT_scale=g_scales[:, bt, batch],
                        rhs=w_codes[:, first : first + 2 * ROW_COLS].bitcast(E4M3X4),
                        rhs_scale=w_scales[:, first : first + 2 * ROW_COLS],
                        start=(i == windows[0]),
                        stop=(i == windows[-1]),
                    )
            return banks

        held = {}
        written = 0
        for j in COLUMN_ORDER:
            held[j] = min(KW, max(0, written - j))
            written = max(written, j + KW)

        def empty(unit, banks, acc, flag):
            j = COLUMN_ORDER[unit // B_TILES]
            go = None
            if flag:
                go = flags.tile([P, 1], F32, tag="go", name="go")
                nc.vector.tensor_scalar(
                    out=go[:], in0=banks[0][:, 0:1], scalar1=1.0, scalar2=1.0, op0=MIN, op1=MAX
                )
            for rp in range(ROW_PAIRS):
                rows = min(2, H - 2 * rp)
                product = banks[rp][:].rearrange("p (r c v) -> p r v c", r=2, v=KW)[:, 0:rows]
                target = acc[:, 2 * rp : 2 * rp + rows, j : j + KW, :]
                if held[j] > 0:
                    nc.vector.tensor_tensor(
                        out=target[:, :, 0 : held[j], :],
                        in0=product[:, :, 0 : held[j], :],
                        in1=target[:, :, 0 : held[j], :],
                        op=ADD,
                    )
                if held[j] < KW:
                    nc.scalar.copy(
                        out=target[:, :, held[j] : KW, :], in_=product[:, :, held[j] : KW, :]
                    )
            return go

        def finish(bt, acc):
            first = 0
            for engine, count in FINISH_SHARES:
                channels = slice(first, first + count)
                first += count
                if engine == "scalar":
                    result = raw.tile([P, count, H * W], F32, tag="raw", name="result")
                else:
                    result = grouped.tile(
                        [P, count, H * W], F32, tag="grouped", name="result", align_bytes=64
                    )
                source = acc[:, :, :, channels].rearrange("p h w (g c) -> p g (h w) c", c=LINE)
                target = result[:].rearrange("p (g c) s -> p g s c", c=LINE)
                if engine == "vector":
                    nc.vector.tensor_copy(out=target, in_=source)
                else:
                    nc.scalar.copy(out=target, in_=source)
                nc.sync.dma_start(
                    out=out[bt * P : (bt + 1) * P, channels].rearrange("b c h w -> b (c h w)"),
                    in_=result[:].rearrange("p c s -> p (c s)"),
                )

        g_raws = {0: load_grad(0)}
        w_raws = {0: load_weight(0), 1: load_weight(1)}
        w_groupeds = {0: regroup_weight(0, w_raws[0], None)}
        go = None
        g_halves = {}
        banks_of = {}
        sums = {}
        multiply_step = [n + (MULTIPLY_LAG if n < B_TILES else MULTIPLY_LAG - 1) for n in range(UNITS)]
        for step in range(multiply_step[-1] + 2):
            for unit in [n for n in range(UNITS) if multiply_step[n] + 1 == step]:
                bt = unit % B_TILES
                if unit < B_TILES:
                    sums[bt] = big.tile([P, H, W, C], F32, tag="big", name="acc")
                go = empty(unit, banks_of[unit], sums[bt], GPSIMD_FROM <= step + 1 < MATRICES)
                if unit >= UNITS - B_TILES:
                    finish(bt, sums[bt])
            if 1 <= step <= 2 * B_TILES:
                bt, half = divmod(step - 1, 2)
                quantise_grad(bt, half, g_halves[bt][half])
            if step % 2 == 0:
                bt = step // 2
                if bt + 1 < B_TILES:
                    g_raws[bt + 1] = load_grad(bt + 1)
                for k in (step + 2, step + 3):
                    if k < MATRICES:
                        w_raws[k] = load_weight(k)
                if bt < B_TILES:
                    g_halves[bt] = turn_grad(g_raws[bt])
            if step + 1 < MATRICES:
                w_groupeds[step + 1] = regroup_weight(step + 1, w_raws[step + 1], go)
            if step < MATRICES:
                quantise_weight(step, w_groupeds[step])
            for unit in [n for n in range(UNITS) if multiply_step[n] == step]:
                if unit == AHEAD_UNIT:
                    multiply(unit, ROWS - 1, ROWS - 1, banks_of[unit])
                else:
                    banks_of[unit] = multiply(unit, 0, ROWS - 1, {})
            if step + 1 == multiply_step[AHEAD_UNIT]:
                banks_of[AHEAD_UNIT] = multiply(AHEAD_UNIT, 0, ROWS - 2, {})
